import numpy as np
import ml_dtypes

BF16 = ml_dtypes.bfloat16


def bf(x):
    return np.asarray(x, np.float32).astype(BF16)


def f32(x):
    return np.asarray(x, np.float32)


def f64(x):
    return np.asarray(x).astype(np.float64)


def striped(idx):
    return np.tile(idx.reshape(-1, 16).T, (8, 1))


C, S, N, B, Q = 256, 256, 512, 128, 16


def setup_inputs():
    return {"scales": f32(0.05 + 0.1 * np.random.uniform(size=(C, S))), "wint": f32(np.random.choice(Q, size=(C, N))), "z": f32(7.0 + np.random.uniform(size=(C, 1))), "x": bf(0.25 * np.random.standard_normal((N, B))), "offs": striped(np.random.permutation(np.tile(np.arange(S), 2))[:N])}


def reference(scales, wint, z, x, offs):
    idx = offs[:16].T.reshape(-1)
    W = f64(scales)[:, idx] * (f64(wint) - f64(z))
    return W @ f64(x)

@@ -1,0 +1,65 @@
+import concourse.mybir as mybir
+from concourse.masks import make_identity
+
+F32, BF16, U16 = mybir.dt.float32, mybir.dt.bfloat16, mybir.dt.uint16
+SUBTRACT, MULT = mybir.AluOpType.subtract, mybir.AluOpType.mult
+COPY = mybir.ActivationFunctionType.Copy
+
+P = 128
+C, S, N, B = 256, 256, 512, 128
+C_BLOCKS = C // P
+J_BLOCKS = N // P
+PIECE = S
+
+FLOPS = 2 * C * N * B
+
+
+def tile_mpqlinearbase_kernel(tc, scales, wint, z, x, offs, out):
+    nc = tc.nc
+    with tc.tile_pool(name="held", bufs=1) as held, tc.psum_pool(name="psum", bufs=1) as psum:
+        offsets = held.tile([P, N // 16], U16, name="offsets")
+        nc.sync.dma_start(offsets[:], offs)
+        tables, zero_points, ints = [], [], []
+        for cb in range(C_BLOCKS):
+            rows = slice(cb * P, (cb + 1) * P)
+            tables.append(held.tile([P, S], F32, name=f"table{cb}"))
+            zero_points.append(held.tile([P, 1], F32, name=f"zero_point{cb}"))
+            ints.append(held.tile([P, N], F32, name=f"ints{cb}"))
+            nc.scalar.dma_start(zero_points[cb][:], z[rows, :])
+            nc.sync.dma_start(tables[cb][:], scales[rows, :])
+            nc.scalar.dma_start(ints[cb][:], wint[rows, :])
+        x_sb = held.tile([P, J_BLOCKS, B], BF16, name="x_sb")
+        nc.gpsimd.dma_start(x_sb[:], x.rearrange("(jb p) b -> p jb b", p=P))
+
+        identity = held.tile([P, P], F32, name="identity")
+        make_identity(nc, identity[:])
+
+        for cb in range(C_BLOCKS):
+            shifted = held.tile([P, N], F32, name=f"shifted{cb}")
+            nc.vector.tensor_scalar(shifted[:], ints[cb][:], zero_points[cb][:], None, SUBTRACT)
+            weights = held.tile([P, N], F32, name=f"weights{cb}")
+            for first in range(0, N, PIECE):
+                picked = tables[cb][:].indirect(offsets[:, first // 16 : (first + PIECE) // 16])
+                nc.vector.tensor_tensor(
+                    weights[:, first : first + PIECE], picked, shifted[:, first : first + PIECE], MULT
+                )
+
+            flipped_ps = psum.tile([P, N], F32, name=f"flipped_ps{cb}")
+            for jb in range(J_BLOCKS):
+                block = slice(jb * P, (jb + 1) * P)
+                nc.tensor.transpose(flipped_ps[:, block], weights[:, block], identity[:])
+            flipped = held.tile([P, N], BF16, name=f"flipped{cb}")
+            nc.scalar.activation(flipped[:], flipped_ps[:], COPY)
+
+            out_ps = psum.tile([P, B], F32, name=f"out_ps{cb}")
+            for jb in range(J_BLOCKS):
+                nc.tensor.matmul(
+                    out_ps[:],
+                    flipped[:, jb * P : (jb + 1) * P],
+                    x_sb[:, jb, :],
+                    start=(jb == 0),
+                    stop=(jb == J_BLOCKS - 1),
+                )
+            result = held.tile([P, B], F32, name=f"result{cb}")
+            nc.scalar.activation(result[:], out_ps[:], COPY)
+            nc.sync.dma_start(out[cb * P : (cb + 1) * P, :], result[:])

@@ -9,14 +9,21 @@ P = 128
 C, S, N, B = 256, 256, 512, 128
 C_BLOCKS = C // P
 J_BLOCKS = N // P
-PIECE = S
 
 FLOPS = 2 * C * N * B
 
 
 def tile_mpqlinearbase_kernel(tc, scales, wint, z, x, offs, out):
     nc = tc.nc
-    with tc.tile_pool(name="held", bufs=1) as held, tc.psum_pool(name="psum", bufs=1) as psum:
+    with (
+        tc.tile_pool(name="held", bufs=1) as held,
+        tc.tile_pool(name="ring", bufs=4) as ring,
+        tc.psum_pool(name="flip", bufs=4) as flip,
+        tc.psum_pool(name="acc", bufs=1) as acc,
+    ):
+        identity = held.tile([P, P], F32, name="identity")
+        make_identity(nc, identity[:])
+
         offsets = held.tile([P, N // 16], U16, name="offsets")
         nc.sync.dma_start(offsets[:], offs)
         tables, zero_points, ints = [], [], []
@@ -29,37 +36,37 @@ def tile_mpqlinearbase_kernel(tc, scales, wint, z, x, offs, out):
             nc.sync.dma_start(tables[cb][:], scales[rows, :])
             nc.scalar.dma_start(ints[cb][:], wint[rows, :])
         x_sb = held.tile([P, J_BLOCKS, B], BF16, name="x_sb")
-        nc.gpsimd.dma_start(x_sb[:], x.rearrange("(jb p) b -> p jb b", p=P))
+        nc.sync.dma_start(x_sb[:], x.rearrange("(jb p) b -> p jb b", p=P))
 
-        identity = held.tile([P, P], F32, name="identity")
-        make_identity(nc, identity[:])
+        shifted = [held.tile([P, N], F32, name=f"shifted{cb}") for cb in range(C_BLOCKS)]
+        out_ps = [acc.tile([P, B], F32, name=f"out_ps{cb}") for cb in range(C_BLOCKS)]
 
-        for cb in range(C_BLOCKS):
-            shifted = held.tile([P, N], F32, name=f"shifted{cb}")
-            nc.vector.tensor_scalar(shifted[:], ints[cb][:], zero_points[cb][:], None, SUBTRACT)
-            weights = held.tile([P, N], F32, name=f"weights{cb}")
-            for first in range(0, N, PIECE):
-                picked = tables[cb][:].indirect(offsets[:, first // 16 : (first + PIECE) // 16])
-                nc.vector.tensor_tensor(
-                    weights[:, first : first + PIECE], picked, shifted[:, first : first + PIECE], MULT
-                )
-
-            flipped_ps = psum.tile([P, N], F32, name=f"flipped_ps{cb}")
-            for jb in range(J_BLOCKS):
-                block = slice(jb * P, (jb + 1) * P)
-                nc.tensor.transpose(flipped_ps[:, block], weights[:, block], identity[:])
-            flipped = held.tile([P, N], BF16, name=f"flipped{cb}")
+        def make_block(cb, jb):
+            if jb == 0:
+                nc.vector.tensor_scalar(shifted[cb][:], ints[cb][:], zero_points[cb][:], None, SUBTRACT)
+            weights = ring.tile([P, P], F32, name="weights")
+            picked = tables[cb][:].indirect(offsets[:, jb * P // 16 : (jb + 1) * P // 16])
+            nc.vector.tensor_tensor(weights[:], picked, shifted[cb][:, jb * P : (jb + 1) * P], MULT)
+            flipped_ps = flip.tile([P, P], F32, name="flipped_ps")
+            nc.tensor.transpose(flipped_ps[:], weights[:], identity[:])
+            flipped = ring.tile([P, P], BF16, name="flipped")
             nc.scalar.activation(flipped[:], flipped_ps[:], COPY)
+            return flipped
 
-            out_ps = psum.tile([P, B], F32, name=f"out_ps{cb}")
-            for jb in range(J_BLOCKS):
-                nc.tensor.matmul(
-                    out_ps[:],
-                    flipped[:, jb * P : (jb + 1) * P],
-                    x_sb[:, jb, :],
-                    start=(jb == 0),
-                    stop=(jb == J_BLOCKS - 1),
-                )
-            result = held.tile([P, B], F32, name=f"result{cb}")
-            nc.scalar.activation(result[:], out_ps[:], COPY)
-            nc.sync.dma_start(out[cb * P : (cb + 1) * P, :], result[:])
+        def multiply_block(cb, jb, flipped):
+            nc.tensor.matmul(
+                out_ps[cb][:], flipped[:], x_sb[:, jb, :], start=(jb == 0), stop=(jb == J_BLOCKS - 1)
+            )
+            if jb == J_BLOCKS - 1:
+                result = ring.tile([P, B], F32, name="result")
+                nc.scalar.activation(result[:], out_ps[cb][:], COPY)
+                nc.sync.dma_start(out[cb * P : (cb + 1) * P, :], result[:])
+
+        blocks = [(cb, jb) for cb in range(C_BLOCKS) for jb in range(J_BLOCKS)]
+        earlier = None
+        for cb, jb in blocks:
+            flipped = make_block(cb, jb)
+            if earlier is not None:
+                multiply_block(*earlier)
+            earlier = (cb, jb, flipped)
+        multiply_block(*earlier)

@@ -9,6 +9,7 @@ P = 128
 C, S, N, B = 256, 256, 512, 128
 C_BLOCKS = C // P
 J_BLOCKS = N // P
+HALF = N // 2
 
 FLOPS = 2 * C * N * B
 
@@ -34,7 +35,8 @@ def tile_mpqlinearbase_kernel(tc, scales, wint, z, x, offs, out):
             ints.append(held.tile([P, N], F32, name=f"ints{cb}"))
             nc.scalar.dma_start(zero_points[cb][:], z[rows, :])
             nc.sync.dma_start(tables[cb][:], scales[rows, :])
-            nc.scalar.dma_start(ints[cb][:], wint[rows, :])
+            for first in range(0, N, HALF):
+                nc.scalar.dma_start(ints[cb][:, first : first + HALF], wint[rows, first : first + HALF])
         x_sb = held.tile([P, J_BLOCKS, B], BF16, name="x_sb")
         nc.sync.dma_start(x_sb[:], x.rearrange("(jb p) b -> p jb b", p=P))
 
@@ -42,8 +44,11 @@ def tile_mpqlinearbase_kernel(tc, scales, wint, z, x, offs, out):
         out_ps = [acc.tile([P, B], F32, name=f"out_ps{cb}") for cb in range(C_BLOCKS)]
 
         def make_block(cb, jb):
-            if jb == 0:
-                nc.vector.tensor_scalar(shifted[cb][:], ints[cb][:], zero_points[cb][:], None, SUBTRACT)
+            if jb * P % HALF == 0:
+                half = slice(jb * P, jb * P + HALF)
+                nc.vector.tensor_scalar(
+                    shifted[cb][:, half], ints[cb][:, half], zero_points[cb][:], None, SUBTRACT
+                )
             weights = ring.tile([P, P], F32, name="weights")
             picked = tables[cb][:].indirect(offsets[:, jb * P // 16 : (jb + 1) * P // 16])
             nc.vector.tensor_tensor(weights[:], picked, shifted[cb][:, jb * P : (jb + 1) * P], MULT)

@@ -3,7 +3,7 @@ from concourse.masks import make_identity
 
 F32, BF16, U16 = mybir.dt.float32, mybir.dt.bfloat16, mybir.dt.uint16
 SUBTRACT, MULT = mybir.AluOpType.subtract, mybir.AluOpType.mult
-COPY = mybir.ActivationFunctionType.Copy
+COPY, IDENTITY = mybir.ActivationFunctionType.Copy, mybir.ActivationFunctionType.Identity
 
 P = 128
 C, S, N, B = 256, 256, 512, 128
@@ -27,28 +27,38 @@ def tile_mpqlinearbase_kernel(tc, scales, wint, z, x, offs, out):
 
         offsets = held.tile([P, N // 16], U16, name="offsets")
         nc.sync.dma_start(offsets[:], offs)
-        tables, zero_points, ints = [], [], []
+        tables = [held.tile([P, S], F32, name=f"table{cb}") for cb in range(C_BLOCKS)]
+        zero_points = [held.tile([P, 1], F32, name=f"zero_point{cb}") for cb in range(C_BLOCKS)]
+        ints = [held.tile([P, N], F32, name=f"ints{cb}") for cb in range(C_BLOCKS)]
+        x_sb = held.tile([P, J_BLOCKS, B], BF16, name="x_sb")
+        for cb in range(C_BLOCKS):
+            nc.sync.dma_start(zero_points[cb][:], z[cb * P : (cb + 1) * P, :])
         for cb in range(C_BLOCKS):
             rows = slice(cb * P, (cb + 1) * P)
-            tables.append(held.tile([P, S], F32, name=f"table{cb}"))
-            zero_points.append(held.tile([P, 1], F32, name=f"zero_point{cb}"))
-            ints.append(held.tile([P, N], F32, name=f"ints{cb}"))
-            nc.scalar.dma_start(zero_points[cb][:], z[rows, :])
             nc.sync.dma_start(tables[cb][:], scales[rows, :])
             for first in range(0, N, HALF):
-                nc.scalar.dma_start(ints[cb][:, first : first + HALF], wint[rows, first : first + HALF])
-        x_sb = held.tile([P, J_BLOCKS, B], BF16, name="x_sb")
-        nc.sync.dma_start(x_sb[:], x.rearrange("(jb p) b -> p jb b", p=P))
+                nc.sync.dma_start(ints[cb][:, first : first + HALF], wint[rows, first : first + HALF])
+            if cb == 0:
+                nc.sync.dma_start(x_sb[:], x.rearrange("(jb p) b -> p jb b", p=P))
 
         shifted = [held.tile([P, N], F32, name=f"shifted{cb}") for cb in range(C_BLOCKS)]
         out_ps = [acc.tile([P, B], F32, name=f"out_ps{cb}") for cb in range(C_BLOCKS)]
 
-        def make_block(cb, jb):
-            if jb * P % HALF == 0:
-                half = slice(jb * P, jb * P + HALF)
+        minus_z = [held.tile([P, 1], F32, name=f"minus_z{cb}") for cb in range(C_BLOCKS)]
+        for cb in range(C_BLOCKS):
+            nc.scalar.mul(minus_z[cb][:], zero_points[cb][:], -1.0)
+
+        def shift_half(h):
+            cb, first = divmod(h * HALF, N)
+            half = slice(first, first + HALF)
+            if h == 0:
                 nc.vector.tensor_scalar(
                     shifted[cb][:, half], ints[cb][:, half], zero_points[cb][:], None, SUBTRACT
                 )
+            else:
+                nc.scalar.activation(shifted[cb][:, half], ints[cb][:, half], IDENTITY, bias=minus_z[cb][:])
+
+        def make_block(cb, jb):
             weights = ring.tile([P, P], F32, name="weights")
             picked = tables[cb][:].indirect(offsets[:, jb * P // 16 : (jb + 1) * P // 16])
             nc.vector.tensor_tensor(weights[:], picked, shifted[cb][:, jb * P : (jb + 1) * P], MULT)
@@ -65,11 +75,16 @@ def tile_mpqlinearbase_kernel(tc, scales, wint, z, x, offs, out):
             if jb == J_BLOCKS - 1:
                 result = ring.tile([P, B], F32, name="result")
                 nc.scalar.activation(result[:], out_ps[cb][:], COPY)
-                nc.sync.dma_start(out[cb * P : (cb + 1) * P, :], result[:])
+                nc.scalar.dma_start(out[cb * P : (cb + 1) * P, :], result[:])
 
         blocks = [(cb, jb) for cb in range(C_BLOCKS) for jb in range(J_BLOCKS)]
+        blocks_in_half = HALF // P
+        n_halves = len(blocks) // blocks_in_half
+        shift_half(0)
         earlier = None
-        for cb, jb in blocks:
+        for i, (cb, jb) in enumerate(blocks):
+            if i % blocks_in_half == 0 and i // blocks_in_half + 1 < n_halves:
+                shift_half(i // blocks_in_half + 1)
             flipped = make_block(cb, jb)
             if earlier is not None:
                 multiply_block(*earlier)

@@ -10,6 +10,7 @@ C, S, N, B = 256, 256, 512, 128
 C_BLOCKS = C // P
 J_BLOCKS = N // P
 HALF = N // 2
+LEAD = 3
 
 FLOPS = 2 * C * N * B
 
@@ -31,15 +32,25 @@ def tile_mpqlinearbase_kernel(tc, scales, wint, z, x, offs, out):
         zero_points = [held.tile([P, 1], F32, name=f"zero_point{cb}") for cb in range(C_BLOCKS)]
         ints = [held.tile([P, N], F32, name=f"ints{cb}") for cb in range(C_BLOCKS)]
         x_sb = held.tile([P, J_BLOCKS, B], BF16, name="x_sb")
+
+        def load_table(cb):
+            nc.sync.dma_start(tables[cb][:], scales[cb * P : (cb + 1) * P, :])
+
+        def load_half(h):
+            cb, first = divmod(h * HALF, N)
+            nc.sync.dma_start(
+                ints[cb][:, first : first + HALF], wint[cb * P : (cb + 1) * P, first : first + HALF]
+            )
+
         for cb in range(C_BLOCKS):
             nc.sync.dma_start(zero_points[cb][:], z[cb * P : (cb + 1) * P, :])
-        for cb in range(C_BLOCKS):
-            rows = slice(cb * P, (cb + 1) * P)
-            nc.sync.dma_start(tables[cb][:], scales[rows, :])
-            for first in range(0, N, HALF):
-                nc.sync.dma_start(ints[cb][:, first : first + HALF], wint[rows, first : first + HALF])
-            if cb == 0:
-                nc.sync.dma_start(x_sb[:], x.rearrange("(jb p) b -> p jb b", p=P))
+        load_table(0)
+        load_half(0)
+        load_half(1)
+        load_half(2)
+        nc.sync.dma_start(x_sb[:], x.rearrange("(jb p) b -> p jb b", p=P))
+        load_table(1)
+        load_half(3)
 
         shifted = [held.tile([P, N], F32, name=f"shifted{cb}") for cb in range(C_BLOCKS)]
         out_ps = [acc.tile([P, B], F32, name=f"out_ps{cb}") for cb in range(C_BLOCKS)]
@@ -72,21 +83,23 @@ def tile_mpqlinearbase_kernel(tc, scales, wint, z, x, offs, out):
             nc.tensor.matmul(
                 out_ps[cb][:], flipped[:], x_sb[:, jb, :], start=(jb == 0), stop=(jb == J_BLOCKS - 1)
             )
-            if jb == J_BLOCKS - 1:
-                result = ring.tile([P, B], F32, name="result")
-                nc.scalar.activation(result[:], out_ps[cb][:], COPY)
-                nc.scalar.dma_start(out[cb * P : (cb + 1) * P, :], result[:])
 
         blocks = [(cb, jb) for cb in range(C_BLOCKS) for jb in range(J_BLOCKS)]
         blocks_in_half = HALF // P
-        n_halves = len(blocks) // blocks_in_half
-        shift_half(0)
         earlier = None
-        for i, (cb, jb) in enumerate(blocks):
-            if i % blocks_in_half == 0 and i // blocks_in_half + 1 < n_halves:
-                shift_half(i // blocks_in_half + 1)
-            flipped = make_block(cb, jb)
-            if earlier is not None:
-                multiply_block(*earlier)
-            earlier = (cb, jb, flipped)
+        for i in range(-LEAD, len(blocks)):
+            if (i + LEAD) % blocks_in_half == 0 and i + LEAD < len(blocks):
+                shift_half((i + LEAD) // blocks_in_half)
+            if i >= 0:
+                cb, jb = blocks[i]
+                flipped = make_block(cb, jb)
+                if earlier is not None:
+                    multiply_block(*earlier)
+                earlier = (cb, jb, flipped)
         multiply_block(*earlier)
+
+        results = [held.tile([P, B], F32, name=f"result{cb}") for cb in range(C_BLOCKS)]
+        nc.vector.tensor_copy(results[0][:], out_ps[0][:])
+        nc.sync.dma_start(out[0:P, :], results[0][:])
+        nc.scalar.activation(results[1][:], out_ps[1][:], COPY)
+        nc.scalar.dma_start(out[P : 2 * P, :], results[1][:])

@@ -10,7 +10,6 @@ C, S, N, B = 256, 256, 512, 128
 C_BLOCKS = C // P
 J_BLOCKS = N // P
 HALF = N // 2
-LEAD = 3
 
 FLOPS = 2 * C * N * B
 
@@ -32,25 +31,15 @@ def tile_mpqlinearbase_kernel(tc, scales, wint, z, x, offs, out):
         zero_points = [held.tile([P, 1], F32, name=f"zero_point{cb}") for cb in range(C_BLOCKS)]
         ints = [held.tile([P, N], F32, name=f"ints{cb}") for cb in range(C_BLOCKS)]
         x_sb = held.tile([P, J_BLOCKS, B], BF16, name="x_sb")
-
-        def load_table(cb):
-            nc.sync.dma_start(tables[cb][:], scales[cb * P : (cb + 1) * P, :])
-
-        def load_half(h):
-            cb, first = divmod(h * HALF, N)
-            nc.sync.dma_start(
-                ints[cb][:, first : first + HALF], wint[cb * P : (cb + 1) * P, first : first + HALF]
-            )
-
         for cb in range(C_BLOCKS):
-            nc.sync.dma_start(zero_points[cb][:], z[cb * P : (cb + 1) * P, :])
-        load_table(0)
-        load_half(0)
-        load_half(1)
-        load_half(2)
-        nc.sync.dma_start(x_sb[:], x.rearrange("(jb p) b -> p jb b", p=P))
-        load_table(1)
-        load_half(3)
+            nc.scalar.dma_start(zero_points[cb][:], z[cb * P : (cb + 1) * P, :])
+        for cb in range(C_BLOCKS):
+            rows = slice(cb * P, (cb + 1) * P)
+            nc.sync.dma_start(tables[cb][:], scales[rows, :])
+            for first in range(0, N, HALF):
+                nc.sync.dma_start(ints[cb][:, first : first + HALF], wint[rows, first : first + HALF])
+            if cb == 0:
+                nc.sync.dma_start(x_sb[:], x.rearrange("(jb p) b -> p jb b", p=P))
 
         shifted = [held.tile([P, N], F32, name=f"shifted{cb}") for cb in range(C_BLOCKS)]
         out_ps = [acc.tile([P, B], F32, name=f"out_ps{cb}") for cb in range(C_BLOCKS)]
@@ -83,23 +72,21 @@ def tile_mpqlinearbase_kernel(tc, scales, wint, z, x, offs, out):
             nc.tensor.matmul(
                 out_ps[cb][:], flipped[:], x_sb[:, jb, :], start=(jb == 0), stop=(jb == J_BLOCKS - 1)
             )
+            if jb == J_BLOCKS - 1:
+                result = ring.tile([P, B], F32, name="result")
+                nc.scalar.activation(result[:], out_ps[cb][:], COPY)
+                nc.scalar.dma_start(out[cb * P : (cb + 1) * P, :], result[:])
 
         blocks = [(cb, jb) for cb in range(C_BLOCKS) for jb in range(J_BLOCKS)]
         blocks_in_half = HALF // P
+        n_halves = len(blocks) // blocks_in_half
+        shift_half(0)
         earlier = None
-        for i in range(-LEAD, len(blocks)):
-            if (i + LEAD) % blocks_in_half == 0 and i + LEAD < len(blocks):
-                shift_half((i + LEAD) // blocks_in_half)
-            if i >= 0:
-                cb, jb = blocks[i]
-                flipped = make_block(cb, jb)
-                if earlier is not None:
-                    multiply_block(*earlier)
-                earlier = (cb, jb, flipped)
+        for i, (cb, jb) in enumerate(blocks):
+            if i % blocks_in_half == 0 and i // blocks_in_half + 1 < n_halves:
+                shift_half(i // blocks_in_half + 1)
+            flipped = make_block(cb, jb)
+            if earlier is not None:
+                multiply_block(*earlier)
+            earlier = (cb, jb, flipped)
         multiply_block(*earlier)
-
-        results = [held.tile([P, B], F32, name=f"result{cb}") for cb in range(C_BLOCKS)]
-        nc.vector.tensor_copy(results[0][:], out_ps[0][:])
-        nc.sync.dma_start(out[0:P, :], results[0][:])
-        nc.scalar.activation(results[1][:], out_ps[1][:], COPY)
-        nc.scalar.dma_start(out[P : 2 * P, :], results[1][:])

@@ -38,8 +38,7 @@ def tile_mpqlinearbase_kernel(tc, scales, wint, z, x, offs, out):
             nc.sync.dma_start(tables[cb][:], scales[rows, :])
             for first in range(0, N, HALF):
                 nc.sync.dma_start(ints[cb][:, first : first + HALF], wint[rows, first : first + HALF])
-            if cb == 0:
-                nc.sync.dma_start(x_sb[:], x.rearrange("(jb p) b -> p jb b", p=P))
+        nc.sync.dma_start(x_sb[:], x.rearrange("(jb p) b -> p jb b", p=P))
 
         shifted = [held.tile([P, N], F32, name=f"shifted{cb}") for cb in range(C_BLOCKS)]
         out_ps = [acc.tile([P, B], F32, name=f"out_ps{cb}") for cb in range(C_BLOCKS)]

@@ -35,9 +35,9 @@ def tile_mpqlinearbase_kernel(tc, scales, wint, z, x, offs, out):
             nc.scalar.dma_start(zero_points[cb][:], z[cb * P : (cb + 1) * P, :])
         for cb in range(C_BLOCKS):
             rows = slice(cb * P, (cb + 1) * P)
+            nc.sync.dma_start(ints[cb][:, :HALF], wint[rows, :HALF])
             nc.sync.dma_start(tables[cb][:], scales[rows, :])
-            for first in range(0, N, HALF):
-                nc.sync.dma_start(ints[cb][:, first : first + HALF], wint[rows, first : first + HALF])
+            nc.sync.dma_start(ints[cb][:, HALF:], wint[rows, HALF:])
         nc.sync.dma_start(x_sb[:], x.rearrange("(jb p) b -> p jb b", p=P))
 
         shifted = [held.tile([P, N], F32, name=f"shifted{cb}") for cb in range(C_BLOCKS)]

@@ -37,7 +37,11 @@ def tile_mpqlinearbase_kernel(tc, scales, wint, z, x, offs, out):
             rows = slice(cb * P, (cb + 1) * P)
             nc.sync.dma_start(ints[cb][:, :HALF], wint[rows, :HALF])
             nc.sync.dma_start(tables[cb][:], scales[rows, :])
-            nc.sync.dma_start(ints[cb][:, HALF:], wint[rows, HALF:])
+            if cb == 0:
+                for first in range(HALF, N, P):
+                    nc.sync.dma_start(ints[cb][:, first : first + P], wint[rows, first : first + P])
+            else:
+                nc.sync.dma_start(ints[cb][:, HALF:], wint[rows, HALF:])
         nc.sync.dma_start(x_sb[:], x.rearrange("(jb p) b -> p jb b", p=P))
 
         shifted = [held.tile([P, N], F32, name=f"shifted{cb}") for cb in range(C_BLOCKS)]
@@ -54,6 +58,10 @@ def tile_mpqlinearbase_kernel(tc, scales, wint, z, x, offs, out):
                 nc.vector.tensor_scalar(
                     shifted[cb][:, half], ints[cb][:, half], zero_points[cb][:], None, SUBTRACT
                 )
+            elif h == 1:
+                for block_first in range(first, first + HALF, P):
+                    block = slice(block_first, block_first + P)
+                    nc.scalar.activation(shifted[cb][:, block], ints[cb][:, block], IDENTITY, bias=minus_z[cb][:])
             else:
                 nc.scalar.activation(shifted[cb][:, half], ints[cb][:, half], IDENTITY, bias=minus_z[cb][:])
 

@@ -11,6 +11,8 @@ C_BLOCKS = C // P
 J_BLOCKS = N // P
 HALF = N // 2
 
+ALIGN = 256
+
 FLOPS = 2 * C * N * B
 
 
@@ -22,15 +24,15 @@ def tile_mpqlinearbase_kernel(tc, scales, wint, z, x, offs, out):
         tc.psum_pool(name="flip", bufs=4) as flip,
         tc.psum_pool(name="acc", bufs=1) as acc,
     ):
-        identity = held.tile([P, P], F32, name="identity")
+        identity = held.tile([P, P], F32, name="identity", align_bytes=ALIGN)
         make_identity(nc, identity[:])
 
-        offsets = held.tile([P, N // 16], U16, name="offsets")
+        offsets = held.tile([P, N // 16], U16, name="offsets", align_bytes=ALIGN)
         nc.sync.dma_start(offsets[:], offs)
-        tables = [held.tile([P, S], F32, name=f"table{cb}") for cb in range(C_BLOCKS)]
-        zero_points = [held.tile([P, 1], F32, name=f"zero_point{cb}") for cb in range(C_BLOCKS)]
-        ints = [held.tile([P, N], F32, name=f"ints{cb}") for cb in range(C_BLOCKS)]
-        x_sb = held.tile([P, J_BLOCKS, B], BF16, name="x_sb")
+        tables = [held.tile([P, S], F32, name=f"table{cb}", align_bytes=ALIGN) for cb in range(C_BLOCKS)]
+        zero_points = [held.tile([P, 1], F32, name=f"zero_point{cb}", align_bytes=ALIGN) for cb in range(C_BLOCKS)]
+        ints = [held.tile([P, N], F32, name=f"ints{cb}", align_bytes=ALIGN) for cb in range(C_BLOCKS)]
+        x_sb = held.tile([P, J_BLOCKS, B], BF16, name="x_sb", align_bytes=ALIGN)
         for cb in range(C_BLOCKS):
             nc.scalar.dma_start(zero_points[cb][:], z[cb * P : (cb + 1) * P, :])
         for cb in range(C_BLOCKS):
@@ -44,10 +46,10 @@ def tile_mpqlinearbase_kernel(tc, scales, wint, z, x, offs, out):
                 nc.sync.dma_start(ints[cb][:, HALF:], wint[rows, HALF:])
         nc.sync.dma_start(x_sb[:], x.rearrange("(jb p) b -> p jb b", p=P))
 
-        shifted = [held.tile([P, N], F32, name=f"shifted{cb}") for cb in range(C_BLOCKS)]
+        shifted = [held.tile([P, N], F32, name=f"shifted{cb}", align_bytes=ALIGN) for cb in range(C_BLOCKS)]
         out_ps = [acc.tile([P, B], F32, name=f"out_ps{cb}") for cb in range(C_BLOCKS)]
 
-        minus_z = [held.tile([P, 1], F32, name=f"minus_z{cb}") for cb in range(C_BLOCKS)]
+        minus_z = [held.tile([P, 1], F32, name=f"minus_z{cb}", align_bytes=ALIGN) for cb in range(C_BLOCKS)]
         for cb in range(C_BLOCKS):
             nc.scalar.mul(minus_z[cb][:], zero_points[cb][:], -1.0)
 
@@ -66,12 +68,12 @@ def tile_mpqlinearbase_kernel(tc, scales, wint, z, x, offs, out):
                 nc.scalar.activation(shifted[cb][:, half], ints[cb][:, half], IDENTITY, bias=minus_z[cb][:])
 
         def make_block(cb, jb):
-            weights = ring.tile([P, P], F32, name="weights")
+            weights = ring.tile([P, P], F32, name="weights", align_bytes=ALIGN)
             picked = tables[cb][:].indirect(offsets[:, jb * P // 16 : (jb + 1) * P // 16])
             nc.vector.tensor_tensor(weights[:], picked, shifted[cb][:, jb * P : (jb + 1) * P], MULT)
             flipped_ps = flip.tile([P, P], F32, name="flipped_ps")
             nc.tensor.transpose(flipped_ps[:], weights[:], identity[:])
-            flipped = ring.tile([P, P], BF16, name="flipped")
+            flipped = ring.tile([P, P], BF16, name="flipped", align_bytes=ALIGN)
             nc.scalar.activation(flipped[:], flipped_ps[:], COPY)
             return flipped
 
@@ -80,7 +82,7 @@ def tile_mpqlinearbase_kernel(tc, scales, wint, z, x, offs, out):
                 out_ps[cb][:], flipped[:], x_sb[:, jb, :], start=(jb == 0), stop=(jb == J_BLOCKS - 1)
             )
             if jb == J_BLOCKS - 1:
-                result = ring.tile([P, B], F32, name="result")
+                result = ring.tile([P, B], F32, name="result", align_bytes=ALIGN)
                 nc.scalar.activation(result[:], out_ps[cb][:], COPY)
                 nc.scalar.dma_start(out[cb * P : (cb + 1) * P, :], result[:])
 

@@ -49,10 +49,6 @@ def tile_mpqlinearbase_kernel(tc, scales, wint, z, x, offs, out):
         shifted = [held.tile([P, N], F32, name=f"shifted{cb}", align_bytes=ALIGN) for cb in range(C_BLOCKS)]
         out_ps = [acc.tile([P, B], F32, name=f"out_ps{cb}") for cb in range(C_BLOCKS)]
 
-        minus_z = [held.tile([P, 1], F32, name=f"minus_z{cb}", align_bytes=ALIGN) for cb in range(C_BLOCKS)]
-        for cb in range(C_BLOCKS):
-            nc.scalar.mul(minus_z[cb][:], zero_points[cb][:], -1.0)
-
         def shift_half(h):
             cb, first = divmod(h * HALF, N)
             half = slice(first, first + HALF)
@@ -63,9 +59,9 @@ def tile_mpqlinearbase_kernel(tc, scales, wint, z, x, offs, out):
             elif h == 1:
                 for block_first in range(first, first + HALF, P):
                     block = slice(block_first, block_first + P)
-                    nc.scalar.activation(shifted[cb][:, block], ints[cb][:, block], IDENTITY, bias=minus_z[cb][:])
+                    nc.scalar.activation(shifted[cb][:, block], ints[cb][:, block], IDENTITY, bias=zero_points[cb][:], scale=-1.0)
             else:
-                nc.scalar.activation(shifted[cb][:, half], ints[cb][:, half], IDENTITY, bias=minus_z[cb][:])
+                nc.scalar.activation(shifted[cb][:, half], ints[cb][:, half], IDENTITY, bias=zero_points[cb][:], scale=-1.0)
 
         def make_block(cb, jb):
             weights = ring.tile([P, P], F32, name="weights", align_bytes=ALIGN)
@@ -74,7 +70,8 @@ def tile_mpqlinearbase_kernel(tc, scales, wint, z, x, offs, out):
             flipped_ps = flip.tile([P, P], F32, name="flipped_ps")
             nc.tensor.transpose(flipped_ps[:], weights[:], identity[:])
             flipped = ring.tile([P, P], BF16, name="flipped", align_bytes=ALIGN)
-            nc.scalar.activation(flipped[:], flipped_ps[:], COPY)
+            made_by_vector = (cb * N + jb * P) < HALF
+            nc.scalar.activation(flipped[:], flipped_ps[:], COPY, scale=1.0 if made_by_vector else -1.0)
             return flipped
 
         def multiply_block(cb, jb, flipped):

@@ -26,6 +26,9 @@ def tile_mpqlinearbase_kernel(tc, scales, wint, z, x, offs, out):
     ):
         identity = held.tile([P, P], F32, name="identity", align_bytes=ALIGN)
         make_identity(nc, identity[:])
+        table_loader = held.tile([P, 2], F32, name="table_loader", align_bytes=ALIGN)
+        nc.vector.memset(table_loader[:, :1], 0.0)
+        nc.scalar.activation(table_loader[:, 1:], table_loader[:, :1], COPY)
 
         offsets = held.tile([P, N // 16], U16, name="offsets", align_bytes=ALIGN)
         nc.sync.dma_start(offsets[:], offs)
@@ -39,11 +42,7 @@ def tile_mpqlinearbase_kernel(tc, scales, wint, z, x, offs, out):
             rows = slice(cb * P, (cb + 1) * P)
             nc.sync.dma_start(ints[cb][:, :HALF], wint[rows, :HALF])
             nc.sync.dma_start(tables[cb][:], scales[rows, :])
-            if cb == 0:
-                for first in range(HALF, N, P):
-                    nc.sync.dma_start(ints[cb][:, first : first + P], wint[rows, first : first + P])
-            else:
-                nc.sync.dma_start(ints[cb][:, HALF:], wint[rows, HALF:])
+            nc.sync.dma_start(ints[cb][:, HALF:], wint[rows, HALF:])
         nc.sync.dma_start(x_sb[:], x.rearrange("(jb p) b -> p jb b", p=P))
 
         shifted = [held.tile([P, N], F32, name=f"shifted{cb}", align_bytes=ALIGN) for cb in range(C_BLOCKS)]

@@ -48,19 +48,13 @@ def tile_mpqlinearbase_kernel(tc, scales, wint, z, x, offs, out):
         shifted = [held.tile([P, N], F32, name=f"shifted{cb}", align_bytes=ALIGN) for cb in range(C_BLOCKS)]
         out_ps = [acc.tile([P, B], F32, name=f"out_ps{cb}") for cb in range(C_BLOCKS)]
 
-        def shift_half(h):
-            cb, first = divmod(h * HALF, N)
-            half = slice(first, first + HALF)
-            if h == 0:
-                nc.vector.tensor_scalar(
-                    shifted[cb][:, half], ints[cb][:, half], zero_points[cb][:], None, SUBTRACT
-                )
-            elif h == 1:
-                for block_first in range(first, first + HALF, P):
-                    block = slice(block_first, block_first + P)
-                    nc.scalar.activation(shifted[cb][:, block], ints[cb][:, block], IDENTITY, bias=zero_points[cb][:], scale=-1.0)
+        def shift(cb, first, width):
+            columns = slice(first, first + width)
+            source, difference = ints[cb][:, columns], shifted[cb][:, columns]
+            if (cb, first) == (0, 0):
+                nc.vector.tensor_scalar(difference, source, zero_points[cb][:], None, SUBTRACT)
             else:
-                nc.scalar.activation(shifted[cb][:, half], ints[cb][:, half], IDENTITY, bias=zero_points[cb][:], scale=-1.0)
+                nc.scalar.activation(difference, source, IDENTITY, bias=zero_points[cb][:], scale=-1.0)
 
         def make_block(cb, jb):
             weights = ring.tile([P, P], F32, name="weights", align_bytes=ALIGN)
@@ -69,7 +63,7 @@ def tile_mpqlinearbase_kernel(tc, scales, wint, z, x, offs, out):
             flipped_ps = flip.tile([P, P], F32, name="flipped_ps")
             nc.tensor.transpose(flipped_ps[:], weights[:], identity[:])
             flipped = ring.tile([P, P], BF16, name="flipped", align_bytes=ALIGN)
-            made_by_vector = (cb * N + jb * P) < HALF
+            made_by_vector = (cb, jb) == blocks[0]
             nc.scalar.activation(flipped[:], flipped_ps[:], COPY, scale=1.0 if made_by_vector else -1.0)
             return flipped
 
@@ -83,13 +77,12 @@ def tile_mpqlinearbase_kernel(tc, scales, wint, z, x, offs, out):
                 nc.scalar.dma_start(out[cb * P : (cb + 1) * P, :], result[:])
 
         blocks = [(cb, jb) for cb in range(C_BLOCKS) for jb in range(J_BLOCKS)]
-        blocks_in_half = HALF // P
-        n_halves = len(blocks) // blocks_in_half
-        shift_half(0)
+        for first in range(0, N, P):
+            shift(0, first, P)
+        for first in range(0, N, HALF):
+            shift(1, first, HALF)
         earlier = None
-        for i, (cb, jb) in enumerate(blocks):
-            if i % blocks_in_half == 0 and i // blocks_in_half + 1 < n_halves:
-                shift_half(i // blocks_in_half + 1)
+        for cb, jb in blocks:
             flipped = make_block(cb, jb)
             if earlier is not None:
                 multiply_block(*earlier)

import concourse.mybir as mybir
from concourse.masks import make_identity

F32, BF16, U16 = mybir.dt.float32, mybir.dt.bfloat16, mybir.dt.uint16
SUBTRACT, MULT = mybir.AluOpType.subtract, mybir.AluOpType.mult
COPY, IDENTITY = mybir.ActivationFunctionType.Copy, mybir.ActivationFunctionType.Identity

P = 128
C, S, N, B = 256, 256, 512, 128
C_BLOCKS = C // P
J_BLOCKS = N // P
HALF = N // 2

ALIGN = 256

FLOPS = 2 * C * N * B


def tile_mpqlinearbase_kernel(tc, scales, wint, z, x, offs, out):
    nc = tc.nc
    with (
        tc.tile_pool(name="held", bufs=1) as held,
        tc.tile_pool(name="ring", bufs=4) as ring,
        tc.psum_pool(name="flip", bufs=4) as flip,
        tc.psum_pool(name="acc", bufs=1) as acc,
    ):
        identity = held.tile([P, P], F32, name="identity", align_bytes=ALIGN)
        make_identity(nc, identity[:])
        table_loader = held.tile([P, 2], F32, name="table_loader", align_bytes=ALIGN)
        nc.vector.memset(table_loader[:, :1], 0.0)
        nc.scalar.activation(table_loader[:, 1:], table_loader[:, :1], COPY)

        offsets = held.tile([P, N // 16], U16, name="offsets", align_bytes=ALIGN)
        nc.sync.dma_start(offsets[:], offs)
        tables = [held.tile([P, S], F32, name=f"table{cb}", align_bytes=ALIGN) for cb in range(C_BLOCKS)]
        zero_points = [held.tile([P, 1], F32, name=f"zero_point{cb}", align_bytes=ALIGN) for cb in range(C_BLOCKS)]
        ints = [held.tile([P, N], F32, name=f"ints{cb}", align_bytes=ALIGN) for cb in range(C_BLOCKS)]
        x_sb = held.tile([P, J_BLOCKS, B], BF16, name="x_sb", align_bytes=ALIGN)
        for cb in range(C_BLOCKS):
            nc.scalar.dma_start(zero_points[cb][:], z[cb * P : (cb + 1) * P, :])
        for cb in range(C_BLOCKS):
            rows = slice(cb * P, (cb + 1) * P)
            nc.sync.dma_start(ints[cb][:, :HALF], wint[rows, :HALF])
            nc.sync.dma_start(tables[cb][:], scales[rows, :])
            nc.sync.dma_start(ints[cb][:, HALF:], wint[rows, HALF:])
        nc.sync.dma_start(x_sb[:], x.rearrange("(jb p) b -> p jb b", p=P))

        shifted = [held.tile([P, N], F32, name=f"shifted{cb}", align_bytes=ALIGN) for cb in range(C_BLOCKS)]
        out_ps = [acc.tile([P, B], F32, name=f"out_ps{cb}") for cb in range(C_BLOCKS)]

        def shift(cb, first, width):
            columns = slice(first, first + width)
            source, difference = ints[cb][:, columns], shifted[cb][:, columns]
            if (cb, first) == (0, 0):
                nc.vector.tensor_scalar(difference, source, zero_points[cb][:], None, SUBTRACT)
            else:
                nc.scalar.activation(difference, source, IDENTITY, bias=zero_points[cb][:], scale=-1.0)

        def make_block(cb, jb):
            weights = ring.tile([P, P], F32, name="weights", align_bytes=ALIGN)
            picked = tables[cb][:].indirect(offsets[:, jb * P // 16 : (jb + 1) * P // 16])
            nc.vector.tensor_tensor(weights[:], picked, shifted[cb][:, jb * P : (jb + 1) * P], MULT)
            flipped_ps = flip.tile([P, P], F32, name="flipped_ps")
            nc.tensor.transpose(flipped_ps[:], weights[:], identity[:])
            flipped = ring.tile([P, P], BF16, name="flipped", align_bytes=ALIGN)
            made_by_vector = (cb, jb) == blocks[0]
            nc.scalar.activation(flipped[:], flipped_ps[:], COPY, scale=1.0 if made_by_vector else -1.0)
            return flipped

        def multiply_block(cb, jb, flipped):
            nc.tensor.matmul(
                out_ps[cb][:], flipped[:], x_sb[:, jb, :], start=(jb == 0), stop=(jb == J_BLOCKS - 1)
            )
            if jb == J_BLOCKS - 1:
                result = ring.tile([P, B], F32, name="result", align_bytes=ALIGN)
                nc.scalar.activation(result[:], out_ps[cb][:], COPY)
                nc.scalar.dma_start(out[cb * P : (cb + 1) * P, :], result[:])

        blocks = [(cb, jb) for cb in range(C_BLOCKS) for jb in range(J_BLOCKS)]
        for first in range(0, N, P):
            shift(0, first, P)
        for first in range(0, N, HALF):
            shift(1, first, HALF)
        earlier = None
        for cb, jb in blocks:
            flipped = make_block(cb, jb)
            if earlier is not None:
                multiply_block(*earlier)
            earlier = (cb, jb, flipped)
        multiply_block(*earlier)
